import numpy as np
import ml_dtypes


def mxq(x, axis, fmt="e4m3"):
    dtype, down = {"e4m3": (ml_dtypes.float8_e4m3fn, 7), "e5m2": (ml_dtypes.float8_e5m2, 14)}[fmt]
    v = np.moveaxis(np.asarray(x, np.float32).astype(ml_dtypes.bfloat16).astype(np.float64), axis, -1)
    blocks = v.reshape(v.shape[:-1] + (-1, 32))
    amax = np.abs(blocks).max(-1, keepdims=True)
    byte = np.maximum(np.where(amax > 0, np.frexp(amax)[1] - 1 + 127, 0) - down, 1)
    scale = np.exp2(byte - 127.0)
    codes = (blocks / scale).astype(np.float32).astype(dtype).astype(np.float64)
    return np.moveaxis((codes * scale).reshape(v.shape), -1, axis)


WIDE = False


def mx_kscale(k):
    if not WIDE:
        return np.ones(k)
    levels = np.array([10, -10, 5, -5, 0])
    a = np.random.permutation(np.resize(levels, k // 512 * 4)).reshape(k // 512, 4)
    idx = np.arange(k)
    return np.exp2(a[idx // 512, idx % 128 // 32])


BF16 = ml_dtypes.bfloat16


def bf(x):
    return np.asarray(x, np.float32).astype(BF16)


def f64(x):
    return np.asarray(x).astype(np.float64)


B, T, D, N, R = 8, 1024, 512, 512, 32

MAX_ATTENTION_SCALE = 1.0
MIN_ATTENTION_SCALE = 0.05
SCALE_GROWTH_RATE = 0.02
G = 4.0
C0 = 12.0


def cloud(rows, u):
    z = np.random.standard_normal((rows, R))
    return (z @ u / np.sqrt(R) + np.random.standard_normal((rows, D))) * (G / np.sqrt(2.0 * D))


def setup_inputs():
    t = mx_kscale(N)
    u = np.random.standard_normal((R, D))
    x = cloud(B * T, u).reshape(B, T, D)
    positions = cloud(N, u)
    c = C0 * (1.0 + 0.03 * np.random.standard_normal(N)) - np.log(t)
    sign = np.where(np.random.standard_normal(N) < 0.0, -1.0, 1.0)
    temperature = sign * (np.sqrt(2.0) * G / c / MIN_ATTENTION_SCALE - 0.1)
    values = np.random.standard_normal((N, D)) * 0.15 * np.sqrt(N) * (t.mean() / t)[:, None]
    return {"x": bf(x), "positions": bf(positions), "values": bf(values), "temperature": bf(temperature)}


def reference(x, positions, values, temperature):
    x, positions, values, temperature = f64(x), f64(positions), f64(values), f64(temperature)
    Bb, Tt, Dd = x.shape
    ages = np.zeros((positions.shape[0],))
    attention_scale = MIN_ATTENTION_SCALE + (MAX_ATTENTION_SCALE - MIN_ATTENTION_SCALE) * (1.0 - np.exp(-SCALE_GROWTH_RATE * ages))
    x_flat = x.reshape(-1, Dd)
    x2 = np.sum(x_flat * x_flat, axis=-1, keepdims=True)
    p2 = np.sum(positions * positions, axis=-1)[None, :]
    sq = x2 + p2 - 2.0 * (mxq(x_flat, 1, "e4m3") @ mxq(positions, 1, "e4m3").T)
    dists = np.sqrt(np.maximum(sq, 0.0))
    effective_temp = (np.abs(temperature) + 0.1) * attention_scale
    weights = np.exp(-dists / effective_temp[None, :])
    weights = weights / (np.sum(weights, axis=-1, keepdims=True) + 1e-8)
    out = mxq(weights, 1, "e4m3") @ mxq(values, 0, "e4m3")
    return out.reshape(Bb, Tt, Dd)

@@ -1,0 +1,312 @@
+import math
+from contextlib import ExitStack
+
+import concourse.mybir as mybir
+from concourse.masks import make_identity
+
+F32 = mybir.dt.float32
+BF16 = mybir.dt.bfloat16
+U32 = mybir.dt.uint32
+U8 = mybir.dt.uint8
+FP8X4 = mybir.dt.float8_e4m3fn_x4
+ALU = mybir.AluOpType
+ACT = mybir.ActivationFunctionType
+
+P = 128
+D = 512
+N = 512
+ROWS = 8192
+NT = ROWS // P
+NP = NT // 2
+FLOPS = 2 * 2 * ROWS * D * N
+
+XTB = 3
+SB = 8 - XTB
+NXG = 2
+NXC = 4
+NW = 3
+NO = 3
+PRE = 3
+A_XT = 3
+A_QX = 2
+A_MM = 1
+A_X2 = 2
+L_I2 = 1
+L_SQ = 2
+A_EX = 3
+A_R = 2
+A_V5 = 1
+L_C1 = 1
+L_Q1 = 1
+L_OUT = 2
+TINY = 1.0e-30
+
+
+def xc_on_scalar(j):
+    return j % 6 != 0
+
+
+def tile_multiscalegeometricattention_t_kernel(tc, x, positions, values, temperature, out):
+    nc = tc.nc
+    xv = x.flatten_outer_dims().rearrange("(p t) d -> p t d", t=NT)
+    ov = out.flatten_outer_dims().rearrange("(p t) d -> p t d", t=NT)
+    with ExitStack() as ctx:
+        sb = ctx.enter_context(tc.tile_pool(name="sb", bufs=1))
+        ps = ctx.enter_context(tc.psum_pool(name="ps", bufs=1))
+        ctx.enter_context(tc.manual_schedule())
+
+        x_sb = sb.tile([P, 8, 4, D], BF16, name="x_sb")
+        v = sb.tile([P, NT, N], F32, name="v")
+        xg = sb.tile([P, NXG, 1024], BF16, name="xg", align_bytes=64)
+        xc = sb.tile([P, NXC, 256], U32, name="xc", align_bytes=64)
+        xs = sb.tile([P, NXC, 256], U8, name="xs", align_bytes=64)
+        posc = sb.tile([P, N], U32, name="posc", align_bytes=64)
+        poss = sb.tile([P, N], U8, name="poss", align_bytes=64)
+        valc = sb.tile([P, D], U32, name="valc", align_bytes=64)
+        vals = sb.tile([P, D], U8, name="vals", align_bytes=64)
+        pos_sb = sb.tile([P, 4, D], BF16, name="pos_sb")
+        val_sb = sb.tile([P, 4, D], BF16, name="val_sb")
+        vg = sb.tile([P, 4 * D], BF16, name="vg", align_bytes=64)
+        wb = sb.tile([P, NW, 2, N], BF16, name="wb")
+        wg = sb.tile([P, NW, 1024], BF16, name="wg", align_bytes=64)
+        wc = sb.tile([P, NW, 256], U32, name="wc", align_bytes=64)
+        ws = sb.tile([P, NW, 256], U8, name="ws", align_bytes=64)
+        ob = sb.tile([P, NO, 2, D], F32, name="ob")
+        x2h = sb.tile([P, NT], F32, name="x2h")
+        sums = sb.tile([P, NT], F32, name="sums")
+        rr = sb.tile([P, NT], F32, name="rr")
+        ra = sb.tile([P, NT], F32, name="ra")
+        p2h = sb.tile([P, 4], F32, name="p2h")
+        t_bf = sb.tile([P, 4], BF16, name="t_bf")
+        t_a = sb.tile([P, 4], F32, name="t_a")
+        t_b = sb.tile([P, 4], F32, name="t_b")
+        idf = sb.tile([P, P], F32, name="idf")
+        idb = sb.tile([P, P], BF16, name="idb")
+        rep_p = sb.tile([P, 4, P], F32, name="rep_p")
+        rep_g = sb.tile([P, 4, P], F32, name="rep_g")
+        p2hb = sb.tile([P, N], F32, name="p2hb")
+        neggb = sb.tile([P, N], F32, name="neggb")
+        junk = sb.tile([P, D], BF16, name="junk")
+        one = sb.tile([P, 1], F32, name="one")
+        one2 = sb.tile([P, 1], F32, name="one2")
+        banks = [ps.tile([P, 512], F32, name="bank%d" % b) for b in range(8)]
+
+        x32 = x_sb[:].bitcast(F32)
+        xg32 = xg[:].bitcast(F32)
+        pos32 = pos_sb[:].bitcast(F32)
+        half = math.sqrt(0.5)
+
+        def load_x(c):
+            if c < NT // 4:
+                nc.sync.dma_start(out=x_sb[:, c % 8, :, :], in_=xv[:, 4 * c : 4 * c + 4, :])
+
+        def sq_norm(t):
+            if 0 <= t < NT:
+                nc.scalar.activation(
+                    out=junk[:], in_=x_sb[:, (t // 4) % 8, t % 4, :], func=ACT.Square, scale=half,
+                    accum_out=x2h[:, t : t + 1],
+                )
+
+        def word_transposes(bank, src32):
+            for i in range(2):
+                for u in range(2):
+                    q = 2 * i + u
+                    nc.tensor.transpose(bank[:, q * P : (q + 1) * P], src32(i)[:, u * P : (u + 1) * P], idf[:])
+
+        def word_copy(bank, slot, on_scalar):
+            src = bank[:].rearrange("p (i u r) -> p i r u", i=2, u=2)
+            dst = xg32[:, slot, :].rearrange("p (i r u) -> p i r u", i=2, u=2)
+            if on_scalar:
+                nc.scalar.copy(out=dst, in_=src)
+            else:
+                nc.vector.tensor_copy(out=dst, in_=src)
+
+        def xt(j):
+            if 0 <= j < NP:
+                word_transposes(banks[j % XTB], lambda i: x32[:, (j // 2) % 8, (2 * j + i) % 4, :])
+
+        def xcopy(j, on_scalar):
+            if 0 <= j < NP and xc_on_scalar(j) == on_scalar:
+                word_copy(banks[j % XTB], j % NXG, on_scalar)
+
+        def qx(j):
+            if 0 <= j < NP:
+                nc.vector.quantize_mx(out=xc[:, j % NXC, :].bitcast(FP8X4), scales=xs[:, j % NXC, :], in_=xg[:, j % NXG, :])
+
+        def mm1(j):
+            if 0 <= j < NP:
+                for i in range(2):
+                    t = 2 * j + i
+                    nc.tensor.matmul_mx(
+                        out=banks[XTB + t % SB][:],
+                        lhsT=xc[:, j % NXC, i * P : (i + 1) * P].bitcast(FP8X4),
+                        lhsT_scale=xs[:, j % NXC, i * P : (i + 1) * P],
+                        rhs=posc[:].bitcast(FP8X4),
+                        rhs_scale=poss[:],
+                        start=True,
+                        stop=True,
+                    )
+
+        def i1(j):
+            if 0 <= j < NP:
+                for t in (2 * j, 2 * j + 1):
+                    nc.vector.scalar_tensor_tensor(
+                        out=v[:, t, :], in0=banks[XTB + t % SB][:], scalar=x2h[:, t : t + 1], in1=p2hb[:],
+                        op0=ALU.subtract, op1=ALU.subtract,
+                    )
+
+        def i2(j):
+            if 0 <= j < NP:
+                nc.vector.scalar_tensor_tensor(
+                    out=v[:, 2 * j : 2 * j + 2, :], in0=v[:, 2 * j : 2 * j + 2, :], scalar=-TINY,
+                    in1=neggb[:].unsqueeze(1).to_broadcast([P, 2, N]), op0=ALU.min, op1=ALU.mult,
+                )
+
+        def sq(j):
+            if 0 <= j < NP:
+                nc.scalar.activation(out=v[:, 2 * j : 2 * j + 2, :], in_=v[:, 2 * j : 2 * j + 2, :], func=ACT.Sqrt)
+
+        def ex(j):
+            if 0 <= j < NP:
+                for t in (2 * j, 2 * j + 1):
+                    nc.scalar.activation(
+                        out=v[:, t, :], in_=v[:, t, :], func=ACT.Exp, scale=-1.0, accum_out=sums[:, t : t + 1]
+                    )
+
+        def r_add(j):
+            if 0 <= j < NP:
+                nc.vector.tensor_scalar_add(out=ra[:, 2 * j : 2 * j + 2], in0=sums[:, 2 * j : 2 * j + 2], scalar1=1.0e-8)
+
+        def r_rec(j):
+            if 0 <= j < NP:
+                nc.vector.reciprocal(out=rr[:, 2 * j : 2 * j + 2], in_=ra[:, 2 * j : 2 * j + 2])
+
+        def v5(j):
+            if 0 <= j < NP:
+                for i in range(2):
+                    t = 2 * j + i
+                    nc.vector.tensor_scalar_mul(out=wb[:, j % NW, i, :], in0=v[:, t, :], scalar1=rr[:, t : t + 1])
+
+        def wt(j):
+            if 0 <= j < NP:
+                bank = banks[j % XTB][:].bitcast(BF16)
+                for i in range(2):
+                    for c in range(4):
+                        q = 4 * i + c
+                        nc.tensor.transpose(bank[:, q * P : (q + 1) * P], wb[:, j % NW, i, c * P : (c + 1) * P], idb[:])
+
+        def c1(j):
+            if 0 <= j < NP:
+                src = banks[j % XTB][:].bitcast(BF16).rearrange("p (i c r) -> p i r c", i=2, c=4)
+                dst = wg[:, j % NW, :].rearrange("p (i r c) -> p i r c", i=2, c=4)
+                nc.vector.tensor_copy(out=dst, in_=src)
+
+        def q1(j):
+            if 0 <= j < NP:
+                nc.vector.quantize_mx(out=wc[:, j % NW, :].bitcast(FP8X4), scales=ws[:, j % NW, :], in_=wg[:, j % NW, :])
+
+        def mm2(j):
+            if 0 <= j < NP:
+                for i in range(2):
+                    t = 2 * j + i
+                    nc.tensor.matmul_mx(
+                        out=banks[XTB + t % SB][:],
+                        lhsT=wc[:, j % NW, i * P : (i + 1) * P].bitcast(FP8X4),
+                        lhsT_scale=ws[:, j % NW, i * P : (i + 1) * P],
+                        rhs=valc[:].bitcast(FP8X4),
+                        rhs_scale=vals[:],
+                        start=True,
+                        stop=True,
+                    )
+
+        def outc(j):
+            if 0 <= j < NP:
+                for i in range(2):
+                    t = 2 * j + i
+                    nc.scalar.copy(out=ob[:, j % NO, i, :], in_=banks[XTB + t % SB][:])
+
+        def store(j):
+            if 0 <= j < NP:
+                nc.sync.dma_start(out=ov[:, 2 * j : 2 * j + 2, :], in_=ob[:, j % NO, :, :])
+
+        nc.vector.memset(one[:], 1.0)
+        nc.scalar.dma_start(out=t_bf[:], in_=temperature.rearrange("(p c) -> p c", c=4))
+        nc.scalar.activation(out=one2[:], in_=one[:], func=ACT.Sqrt)
+        nc.sync.dma_start(out=pos_sb[:], in_=positions.rearrange("(p c) d -> p c d", c=4))
+        make_identity(nc, idf[:])
+        make_identity(nc, idb[:])
+        for c in range(8):
+            load_x(c)
+        nc.sync.dma_start(out=val_sb[:], in_=values.rearrange("(p c) d -> p c d", c=4))
+
+        nc.vector.tensor_copy(out=t_a[:], in_=t_bf[:])
+        nc.vector.tensor_scalar_mul(out=t_b[:], in0=t_a[:], scalar1=-1.0)
+        nc.vector.tensor_tensor(out=t_a[:], in0=t_a[:], in1=t_b[:], op=ALU.max)
+        nc.vector.tensor_scalar(out=t_a[:], in0=t_a[:], scalar1=0.1, scalar2=0.05, op0=ALU.add, op1=ALU.mult)
+        nc.vector.tensor_tensor(out=t_a[:], in0=t_a[:], in1=t_a[:], op=ALU.mult)
+        nc.vector.reciprocal(out=t_b[:], in_=t_a[:])
+        nc.vector.tensor_scalar_mul(out=t_b[:], in0=t_b[:], scalar1=-2.0)
+        nc.vector.tensor_copy(out=rep_g[:], in_=t_b[:].unsqueeze(2).to_broadcast([P, 4, P]))
+        for c in range(4):
+            nc.tensor.transpose(banks[6][:, c * P : (c + 1) * P], rep_g[:, c, :], idf[:])
+        nc.vector.tensor_copy(out=neggb[:], in_=banks[6][:])
+
+        for h in range(2):
+            word_transposes(banks[h], lambda i: pos32[:, 2 * h + i, :])
+        for c in range(4):
+            nc.scalar.activation(out=junk[:], in_=pos_sb[:, c, :], func=ACT.Square, scale=half, accum_out=p2h[:, c : c + 1])
+        for h in range(2):
+            word_copy(banks[h], h, False)
+        for h in range(2):
+            nc.vector.quantize_mx(
+                out=posc[:, h * 256 : (h + 1) * 256].bitcast(FP8X4), scales=poss[:, h * 256 : (h + 1) * 256], in_=xg[:, h, :]
+            )
+        for t in range(2 * A_X2):
+            sq_norm(t)
+        nc.vector.tensor_copy(out=rep_p[:], in_=p2h[:].unsqueeze(2).to_broadcast([P, 4, P]))
+        for c in range(4):
+            nc.tensor.transpose(banks[7][:, c * P : (c + 1) * P], rep_p[:, c, :], idf[:])
+        nc.vector.tensor_copy(out=p2hb[:], in_=banks[7][:])
+        for j in range(PRE):
+            xt(j)
+            xcopy(j, True)
+            xcopy(j, False)
+            qx(j - 1)
+        for j in range(A_MM):
+            mm1(j)
+
+        for j in range(NP + L_SQ):
+            if j % 2 == 0:
+                load_x(8 + j // 2)
+            if j + A_XT >= PRE:
+                xt(j + A_XT)
+            mm1(j + A_MM)
+            sq_norm(2 * (j + A_X2))
+            sq_norm(2 * (j + A_X2) + 1)
+            if j + A_XT >= PRE:
+                xcopy(j + A_XT, True)
+            sq(j - L_SQ)
+            i1(j)
+            i2(j - L_I2)
+            if j + A_XT >= PRE:
+                xcopy(j + A_XT, False)
+            if j + A_QX >= PRE - 1:
+                qx(j + A_QX)
+            if j == NP:
+                nc.vector.tensor_copy(
+                    out=vg[:].rearrange("p (d c) -> p d c", c=4), in_=val_sb[:].rearrange("p c d -> p d c")
+                )
+            if j == NP + 1:
+                nc.vector.quantize_mx(out=valc[:].bitcast(FP8X4), scales=vals[:], in_=vg[:])
+
+        for j in range(-A_EX, NP + L_OUT + 1):
+            ex(j + A_EX)
+            outc(j - L_OUT)
+            store(j - L_OUT)
+            c1(j - L_C1)
+            r_add(j + A_R)
+            v5(j + A_V5)
+            wt(j + A_V5)
+            r_rec(j + A_R)
+            q1(j - L_Q1)
+            mm2(j - L_Q1)

@@ -46,6 +46,10 @@ def xc_on_scalar(j):
     return j % 6 != 0
 
 
+def out_on_scalar(t):
+    return t % 2 == 0 or t % 8 == 7
+
+
 def tile_multiscalegeometricattention_t_kernel(tc, x, positions, values, temperature, out):
     nc = tc.nc
     xv = x.flatten_outer_dims().rearrange("(p t) d -> p t d", t=NT)
@@ -219,11 +223,16 @@ def tile_multiscalegeometricattention_t_kernel(tc, x, positions, values, tempera
                         stop=True,
                     )
 
-        def outc(j):
+        def outc(j, on_scalar):
             if 0 <= j < NP:
                 for i in range(2):
                     t = 2 * j + i
-                    nc.scalar.copy(out=ob[:, j % NO, i, :], in_=banks[XTB + t % SB][:])
+                    if out_on_scalar(t) != on_scalar:
+                        continue
+                    if on_scalar:
+                        nc.scalar.copy(out=ob[:, j % NO, i, :], in_=banks[XTB + t % SB][:])
+                    else:
+                        nc.vector.tensor_copy(out=ob[:, j % NO, i, :], in_=banks[XTB + t % SB][:])
 
         def store(j):
             if 0 <= j < NP:
@@ -301,9 +310,10 @@ def tile_multiscalegeometricattention_t_kernel(tc, x, positions, values, tempera
 
         for j in range(-A_EX, NP + L_OUT + 1):
             ex(j + A_EX)
-            outc(j - L_OUT)
-            store(j - L_OUT)
+            outc(j - L_OUT, True)
             c1(j - L_C1)
+            outc(j - L_OUT, False)
+            store(j - L_OUT)
             r_add(j + A_R)
             v5(j + A_V5)
             wt(j + A_V5)

@@ -18,32 +18,27 @@ N = 512
 ROWS = 8192
 NT = ROWS // P
 NP = NT // 2
+NG = NT // 4
 FLOPS = 2 * 2 * ROWS * D * N
 
-XTB = 3
-SB = 8 - XTB
-NXG = 2
-NXC = 4
+NX = 7
+LN = 3
+NZ = 2
 NW = 3
-NO = 3
-PRE = 3
-A_XT = 3
-A_QX = 2
-A_MM = 1
-A_X2 = 2
-L_I2 = 1
-L_SQ = 2
+NO = 4
+WT = 3
+SB = 8 - WT
 A_EX = 3
-A_R = 2
-A_V5 = 1
-L_C1 = 1
-L_Q1 = 1
-L_OUT = 2
 TINY = 1.0e-30
+BIG = 3.0e38
 
 
-def xc_on_scalar(j):
-    return j % 6 != 0
+def x_on_scalar(g, h):
+    return h == 1 and g % 2 == 1
+
+
+def v5_on_gpsimd(j):
+    return True
 
 
 def out_on_scalar(t):
@@ -59,18 +54,19 @@ def tile_multiscalegeometricattention_t_kernel(tc, x, positions, values, tempera
         ps = ctx.enter_context(tc.psum_pool(name="ps", bufs=1))
         ctx.enter_context(tc.manual_schedule())
 
-        x_sb = sb.tile([P, 8, 4, D], BF16, name="x_sb")
+        x_sb = sb.tile([P, NX, 4, D], BF16, name="x_sb")
         v = sb.tile([P, NT, N], F32, name="v")
-        xg = sb.tile([P, NXG, 1024], BF16, name="xg", align_bytes=64)
-        xc = sb.tile([P, NXC, 256], U32, name="xc", align_bytes=64)
-        xs = sb.tile([P, NXC, 256], U8, name="xs", align_bytes=64)
+        xg = sb.tile([P, 2, 4 * D], BF16, name="xg", align_bytes=64)
+        xc = sb.tile([P, 2, D], U32, name="xc", align_bytes=64)
+        xs = sb.tile([P, 2, D], U8, name="xs", align_bytes=64)
+        xb = sb.tile([P, 2, D], F32, name="xb")
+        zz = sb.tile([P, NZ, 4, D], F32, name="zz")
         posc = sb.tile([P, N], U32, name="posc", align_bytes=64)
         poss = sb.tile([P, N], U8, name="poss", align_bytes=64)
         valc = sb.tile([P, D], U32, name="valc", align_bytes=64)
         vals = sb.tile([P, D], U8, name="vals", align_bytes=64)
         pos_sb = sb.tile([P, 4, D], BF16, name="pos_sb")
-        val_sb = sb.tile([P, 4, D], BF16, name="val_sb")
-        vg = sb.tile([P, 4 * D], BF16, name="vg", align_bytes=64)
+        pg = sb.tile([P, 4 * D], BF16, name="pg", align_bytes=64)
         wb = sb.tile([P, NW, 2, N], BF16, name="wb")
         wg = sb.tile([P, NW, 1024], BF16, name="wg", align_bytes=64)
         wc = sb.tile([P, NW, 256], U32, name="wc", align_bytes=64)
@@ -85,12 +81,9 @@ def tile_multiscalegeometricattention_t_kernel(tc, x, positions, values, tempera
         t_a = sb.tile([P, 4], F32, name="t_a")
         t_b = sb.tile([P, 4], F32, name="t_b")
         idf = sb.tile([P, P], F32, name="idf")
-        idb = sb.tile([P, P], BF16, name="idb")
-        rep_p = sb.tile([P, 4, P], F32, name="rep_p")
-        rep_g = sb.tile([P, 4, P], F32, name="rep_g")
-        p2hb = sb.tile([P, N], F32, name="p2hb")
-        neggb = sb.tile([P, N], F32, name="neggb")
         junk = sb.tile([P, D], BF16, name="junk")
+        junk_v = sb.tile([P, D], BF16, name="junk_v")
+        p2h_v = sb.tile([P, 2], F32, name="p2h_v")
         one = sb.tile([P, 1], F32, name="one")
         one2 = sb.tile([P, 1], F32, name="one2")
         banks = [ps.tile([P, 512], F32, name="bank%d" % b) for b in range(8)]
@@ -98,17 +91,20 @@ def tile_multiscalegeometricattention_t_kernel(tc, x, positions, values, tempera
         x32 = x_sb[:].bitcast(F32)
         xg32 = xg[:].bitcast(F32)
         pos32 = pos_sb[:].bitcast(F32)
+        pg32 = pg[:].bitcast(F32)
+        wb32 = wb[:].bitcast(F32)
+        wg32 = wg[:].bitcast(F32)
         half = math.sqrt(0.5)
 
-        def load_x(c):
-            if c < NT // 4:
-                nc.sync.dma_start(out=x_sb[:, c % 8, :, :], in_=xv[:, 4 * c : 4 * c + 4, :])
+        def load_x(g):
+            if g < NG:
+                nc.sync.dma_start(out=x_sb[:, g % NX, :, :], in_=xv[:, 4 * g : 4 * g + 4, :])
 
-        def sq_norm(t):
-            if 0 <= t < NT:
+        def sq_norm(g, i):
+            if g < NG:
+                t = 4 * g + i
                 nc.scalar.activation(
-                    out=junk[:], in_=x_sb[:, (t // 4) % 8, t % 4, :], func=ACT.Square, scale=half,
-                    accum_out=x2h[:, t : t + 1],
+                    out=junk[:], in_=x_sb[:, g % NX, i, :], func=ACT.Square, scale=half, accum_out=x2h[:, t : t + 1]
                 )
 
         def word_transposes(bank, src32):
@@ -117,58 +113,94 @@ def tile_multiscalegeometricattention_t_kernel(tc, x, positions, values, tempera
                     q = 2 * i + u
                     nc.tensor.transpose(bank[:, q * P : (q + 1) * P], src32(i)[:, u * P : (u + 1) * P], idf[:])
 
-        def word_copy(bank, slot, on_scalar):
+        def word_copy(dst32, bank, on_scalar=False):
             src = bank[:].rearrange("p (i u r) -> p i r u", i=2, u=2)
-            dst = xg32[:, slot, :].rearrange("p (i r u) -> p i r u", i=2, u=2)
+            dst = dst32.rearrange("p (i r u) -> p i r u", i=2, u=2)
             if on_scalar:
                 nc.scalar.copy(out=dst, in_=src)
             else:
                 nc.vector.tensor_copy(out=dst, in_=src)
 
-        def xt(j):
-            if 0 <= j < NP:
-                word_transposes(banks[j % XTB], lambda i: x32[:, (j // 2) % 8, (2 * j + i) % 4, :])
+        def tbank(g, k):
+            return banks[(3 * g + k) % 2]
 
-        def xcopy(j, on_scalar):
-            if 0 <= j < NP and xc_on_scalar(j) == on_scalar:
-                word_copy(banks[j % XTB], j % NXG, on_scalar)
+        def xbank(g, h):
+            return banks[2 + h] if g == 1 else tbank(g - 1, 1 + h)
 
-        def qx(j):
-            if 0 <= j < NP:
-                nc.vector.quantize_mx(out=xc[:, j % NXC, :].bitcast(FP8X4), scales=xs[:, j % NXC, :], in_=xg[:, j % NXG, :])
+        def xt(g, h):
+            if g < NG:
+                word_transposes(xbank(g, h), lambda i: x32[:, g % NX, 2 * h + i, :])
 
-        def mm1(j):
-            if 0 <= j < NP:
-                for i in range(2):
-                    t = 2 * j + i
+        def xcopy(g, h, on_scalar=None):
+            if g < NG:
+                s = x_on_scalar(g, h)
+                if on_scalar is None or s == on_scalar:
+                    word_copy(xg32[:, g % 2, h * 512 : (h + 1) * 512], xbank(g, h), s)
+
+        def qx(g):
+            if g < NG:
+                nc.vector.quantize_mx(out=xc[:, g % 2, :].bitcast(FP8X4), scales=xs[:, g % 2, :], in_=xg[:, g % 2, :])
+
+        def bc(g):
+            if g < NG:
+                for i in range(4):
+                    t = 4 * g + i
+                    nc.tensor.transpose(
+                        tbank(g, 0)[:, i * P : (i + 1) * P], x2h[:, t : t + 1].to_broadcast([P, P]), idf[:]
+                    )
+
+        def bcopy(g):
+            if g < NG:
+                nc.vector.tensor_copy(out=xb[:, g % 2, :], in_=tbank(g, 0)[:])
+
+        def mm1(g):
+            if g < NG:
+                for q in (2, 3, 0, 1):
                     nc.tensor.matmul_mx(
-                        out=banks[XTB + t % SB][:],
-                        lhsT=xc[:, j % NXC, i * P : (i + 1) * P].bitcast(FP8X4),
-                        lhsT_scale=xs[:, j % NXC, i * P : (i + 1) * P],
-                        rhs=posc[:].bitcast(FP8X4),
-                        rhs_scale=poss[:],
+                        out=banks[2 + q][:],
+                        lhsT=posc[:, q * P : (q + 1) * P].bitcast(FP8X4),
+                        lhsT_scale=poss[:, q * P : (q + 1) * P],
+                        rhs=xc[:, g % 2, :].bitcast(FP8X4),
+                        rhs_scale=xs[:, g % 2, :],
                         start=True,
                         stop=True,
                     )
 
-        def i1(j):
-            if 0 <= j < NP:
-                for t in (2 * j, 2 * j + 1):
-                    nc.vector.scalar_tensor_tensor(
-                        out=v[:, t, :], in0=banks[XTB + t % SB][:], scalar=x2h[:, t : t + 1], in1=p2hb[:],
-                        op0=ALU.subtract, op1=ALU.subtract,
-                    )
-
-        def i2(j):
-            if 0 <= j < NP:
+        def dist(g, q):
+            if g < NG:
                 nc.vector.scalar_tensor_tensor(
-                    out=v[:, 2 * j : 2 * j + 2, :], in0=v[:, 2 * j : 2 * j + 2, :], scalar=-TINY,
-                    in1=neggb[:].unsqueeze(1).to_broadcast([P, 2, N]), op0=ALU.min, op1=ALU.mult,
+                    out=zz[:, g % NZ, q, :], in0=banks[2 + q][:], scalar=(p2h[:, q : q + 1] if q < 2 else p2h_v[:, q - 2 : q - 1]), in1=xb[:, g % 2, :],
+                    op0=ALU.subtract, op1=ALU.subtract,
                 )
 
-        def sq(j):
-            if 0 <= j < NP:
-                nc.scalar.activation(out=v[:, 2 * j : 2 * j + 2, :], in_=v[:, 2 * j : 2 * j + 2, :], func=ACT.Sqrt)
+        def clamp_v(g, q):
+            if g < NG and not (q == 3 and g < NG - 1):
+                nc.vector.tensor_scalar(
+                    out=zz[:, g % NZ, q, :], in0=zz[:, g % NZ, q, :], scalar1=-TINY, scalar2=t_b[:, q : q + 1],
+                    op0=ALU.min, op1=ALU.mult,
+                )
+
+        def clamp_g(g, q):
+            if g < NG and not (q == 3 and g == NG - 1):
+                nc.gpsimd.tensor_scalar(
+                    out=zz[:, g % NZ, q, :], in0=zz[:, g % NZ, q, :], scalar1=-TINY, scalar2=-BIG,
+                    op0=ALU.min, op1=ALU.max,
+                )
+                nc.gpsimd.tensor_scalar(
+                    out=zz[:, g % NZ, q, :], in0=zz[:, g % NZ, q, :], scalar1=t_b[:, q : q + 1], scalar2=1.0,
+                    op0=ALU.mult, op1=ALU.mult,
+                )
+
+        def zt(g, i):
+            if 0 <= g < NG:
+                for q in range(4):
+                    nc.tensor.transpose(
+                        banks[6 + i % 2][:, q * P : (q + 1) * P], zz[:, g % NZ, q, i * P : (i + 1) * P], idf[:]
+                    )
+
+        def sq(g, i):
+            if 0 <= g < NG:
+                nc.scalar.activation(out=v[:, 4 * g + i, :], in_=banks[6 + i % 2][:], func=ACT.Sqrt)
 
         def ex(j):
             if 0 <= j < NP:
@@ -179,31 +211,32 @@ def tile_multiscalegeometricattention_t_kernel(tc, x, positions, values, tempera
 
         def r_add(j):
             if 0 <= j < NP:
-                nc.vector.tensor_scalar_add(out=ra[:, 2 * j : 2 * j + 2], in0=sums[:, 2 * j : 2 * j + 2], scalar1=1.0e-8)
+                nc.gpsimd.tensor_scalar(
+                    out=ra[:, 2 * j : 2 * j + 2], in0=sums[:, 2 * j : 2 * j + 2], scalar1=1.0e-8, scalar2=1.0,
+                    op0=ALU.add, op1=ALU.mult,
+                )
 
         def r_rec(j):
             if 0 <= j < NP:
                 nc.vector.reciprocal(out=rr[:, 2 * j : 2 * j + 2], in_=ra[:, 2 * j : 2 * j + 2])
 
-        def v5(j):
+        def v5(j, i):
             if 0 <= j < NP:
-                for i in range(2):
-                    t = 2 * j + i
-                    nc.vector.tensor_scalar_mul(out=wb[:, j % NW, i, :], in0=v[:, t, :], scalar1=rr[:, t : t + 1])
+                t = 2 * j + i
+                o = wb[:, j % NW, i, :].rearrange("p (u m e) -> p u m e", u=2, e=2)
+                a = v[:, t, :].rearrange("p (u e m) -> p u m e", u=2, e=2)
+                if i == 0 and v5_on_gpsimd(j):
+                    nc.gpsimd.tensor_scalar(out=o, in0=a, scalar1=rr[:, t : t + 1], scalar2=1.0, op0=ALU.mult, op1=ALU.mult)
+                else:
+                    nc.vector.tensor_scalar_mul(out=o, in0=a, scalar1=rr[:, t : t + 1])
 
         def wt(j):
             if 0 <= j < NP:
-                bank = banks[j % XTB][:].bitcast(BF16)
-                for i in range(2):
-                    for c in range(4):
-                        q = 4 * i + c
-                        nc.tensor.transpose(bank[:, q * P : (q + 1) * P], wb[:, j % NW, i, c * P : (c + 1) * P], idb[:])
+                word_transposes(banks[j % WT], lambda i: wb32[:, j % NW, i, :])
 
         def c1(j):
             if 0 <= j < NP:
-                src = banks[j % XTB][:].bitcast(BF16).rearrange("p (i c r) -> p i r c", i=2, c=4)
-                dst = wg[:, j % NW, :].rearrange("p (i r c) -> p i r c", i=2, c=4)
-                nc.vector.tensor_copy(out=dst, in_=src)
+                word_copy(wg32[:, j % NW, :], banks[j % WT], j >= NP - 2)
 
         def q1(j):
             if 0 <= j < NP:
@@ -214,7 +247,7 @@ def tile_multiscalegeometricattention_t_kernel(tc, x, positions, values, tempera
                 for i in range(2):
                     t = 2 * j + i
                     nc.tensor.matmul_mx(
-                        out=banks[XTB + t % SB][:],
+                        out=banks[WT + t % SB][:],
                         lhsT=wc[:, j % NW, i * P : (i + 1) * P].bitcast(FP8X4),
                         lhsT_scale=ws[:, j % NW, i * P : (i + 1) * P],
                         rhs=valc[:].bitcast(FP8X4),
@@ -230,9 +263,9 @@ def tile_multiscalegeometricattention_t_kernel(tc, x, positions, values, tempera
                     if out_on_scalar(t) != on_scalar:
                         continue
                     if on_scalar:
-                        nc.scalar.copy(out=ob[:, j % NO, i, :], in_=banks[XTB + t % SB][:])
+                        nc.scalar.copy(out=ob[:, j % NO, i, :], in_=banks[WT + t % SB][:])
                     else:
-                        nc.vector.tensor_copy(out=ob[:, j % NO, i, :], in_=banks[XTB + t % SB][:])
+                        nc.vector.tensor_copy(out=ob[:, j % NO, i, :], in_=banks[WT + t % SB][:])
 
         def store(j):
             if 0 <= j < NP:
@@ -243,10 +276,8 @@ def tile_multiscalegeometricattention_t_kernel(tc, x, positions, values, tempera
         nc.scalar.activation(out=one2[:], in_=one[:], func=ACT.Sqrt)
         nc.sync.dma_start(out=pos_sb[:], in_=positions.rearrange("(p c) d -> p c d", c=4))
         make_identity(nc, idf[:])
-        make_identity(nc, idb[:])
-        for c in range(8):
-            load_x(c)
-        nc.sync.dma_start(out=val_sb[:], in_=values.rearrange("(p c) d -> p c d", c=4))
+        for g in range(NX):
+            load_x(g)
 
         nc.vector.tensor_copy(out=t_a[:], in_=t_bf[:])
         nc.vector.tensor_scalar_mul(out=t_b[:], in0=t_a[:], scalar1=-1.0)
@@ -255,68 +286,91 @@ def tile_multiscalegeometricattention_t_kernel(tc, x, positions, values, tempera
         nc.vector.tensor_tensor(out=t_a[:], in0=t_a[:], in1=t_a[:], op=ALU.mult)
         nc.vector.reciprocal(out=t_b[:], in_=t_a[:])
         nc.vector.tensor_scalar_mul(out=t_b[:], in0=t_b[:], scalar1=-2.0)
-        nc.vector.tensor_copy(out=rep_g[:], in_=t_b[:].unsqueeze(2).to_broadcast([P, 4, P]))
-        for c in range(4):
-            nc.tensor.transpose(banks[6][:, c * P : (c + 1) * P], rep_g[:, c, :], idf[:])
-        nc.vector.tensor_copy(out=neggb[:], in_=banks[6][:])
 
         for h in range(2):
-            word_transposes(banks[h], lambda i: pos32[:, 2 * h + i, :])
-        for c in range(4):
+            word_transposes(banks[2 + h], lambda i: pos32[:, 2 * h + i, :])
+        xt(0, 0)
+        xt(0, 1)
+        for c in range(2):
             nc.scalar.activation(out=junk[:], in_=pos_sb[:, c, :], func=ACT.Square, scale=half, accum_out=p2h[:, c : c + 1])
+        for i in range(4):
+            sq_norm(0, i)
         for h in range(2):
-            word_copy(banks[h], h, False)
-        for h in range(2):
-            nc.vector.quantize_mx(
-                out=posc[:, h * 256 : (h + 1) * 256].bitcast(FP8X4), scales=poss[:, h * 256 : (h + 1) * 256], in_=xg[:, h, :]
+            word_copy(pg32[:, h * 512 : (h + 1) * 512], banks[2 + h])
+        xcopy(0, 0)
+        xcopy(0, 1)
+        nc.vector.quantize_mx(out=posc[:].bitcast(FP8X4), scales=poss[:], in_=pg[:])
+        bc(0)
+        qx(0)
+        for c in range(2, 4):
+            nc.vector.scalar_tensor_tensor(
+                out=junk_v[:], in0=pos_sb[:, c, :], scalar=0.5, in1=pos_sb[:, c, :], op0=ALU.mult, op1=ALU.mult,
+                accum_out=p2h_v[:, c - 2 : c - 1],
             )
-        for t in range(2 * A_X2):
-            sq_norm(t)
-        nc.vector.tensor_copy(out=rep_p[:], in_=p2h[:].unsqueeze(2).to_broadcast([P, 4, P]))
-        for c in range(4):
-            nc.tensor.transpose(banks[7][:, c * P : (c + 1) * P], rep_p[:, c, :], idf[:])
-        nc.vector.tensor_copy(out=p2hb[:], in_=banks[7][:])
-        for j in range(PRE):
-            xt(j)
-            xcopy(j, True)
-            xcopy(j, False)
-            qx(j - 1)
-        for j in range(A_MM):
-            mm1(j)
+        xt(1, 0)
+        xt(1, 1)
+        bcopy(0)
+        for g in range(1, LN):
+            for i in range(4):
+                sq_norm(g, i)
+            if g == 1:
+                xcopy(1, 1, True)
+        xcopy(1, 0, False)
+        xcopy(1, 1, False)
+        bc(1)
 
-        for j in range(NP + L_SQ):
-            if j % 2 == 0:
-                load_x(8 + j // 2)
-            if j + A_XT >= PRE:
-                xt(j + A_XT)
-            mm1(j + A_MM)
-            sq_norm(2 * (j + A_X2))
-            sq_norm(2 * (j + A_X2) + 1)
-            if j + A_XT >= PRE:
-                xcopy(j + A_XT, True)
-            sq(j - L_SQ)
-            i1(j)
-            i2(j - L_I2)
-            if j + A_XT >= PRE:
-                xcopy(j + A_XT, False)
-            if j + A_QX >= PRE - 1:
-                qx(j + A_QX)
-            if j == NP:
+        for g in range(NG + 1):
+            if g >= 1:
+                load_x(g - 1 + NX)
+            if g == 2:
+                nc.sync.dma_start(out=pos_sb[:], in_=values.rearrange("(p c) d -> p c d", c=4))
+            mm1(g)
+            zt(g - 1, 0)
+            zt(g - 1, 1)
+            xt(g + 2, 0)
+            sq_norm(g + LN, 0)
+            sq(g - 1, 0)
+            sq_norm(g + LN, 1)
+            sq(g - 1, 1)
+            for q in (2, 3):
+                dist(g, q)
+                clamp_g(g, q)
+            bcopy(g + 1)
+            xcopy(g + 2, 0, False)
+            xt(g + 2, 1)
+            zt(g - 1, 2)
+            sq_norm(g + LN, 2)
+            sq(g - 1, 2)
+            dist(g, 0)
+            dist(g, 1)
+            zt(g - 1, 3)
+            sq_norm(g + LN, 3)
+            sq(g - 1, 3)
+            bc(g + 2)
+            qx(g + 1)
+            clamp_v(g, 3)
+            clamp_v(g, 0)
+            xcopy(g + 2, 1, False)
+            clamp_v(g, 1)
+            xcopy(g + 2, 0, True)
+            xcopy(g + 2, 1, True)
+            if g == NG - 1:
                 nc.vector.tensor_copy(
-                    out=vg[:].rearrange("p (d c) -> p d c", c=4), in_=val_sb[:].rearrange("p c d -> p d c")
+                    out=pg[:].rearrange("p (d c) -> p d c", c=4), in_=pos_sb[:].rearrange("p c d -> p d c")
                 )
-            if j == NP + 1:
-                nc.vector.quantize_mx(out=valc[:].bitcast(FP8X4), scales=vals[:], in_=vg[:])
+            if g == NG:
+                nc.vector.quantize_mx(out=valc[:].bitcast(FP8X4), scales=vals[:], in_=pg[:])
 
-        for j in range(-A_EX, NP + L_OUT + 1):
+        for j in range(-A_EX, NP + 3):
             ex(j + A_EX)
-            outc(j - L_OUT, True)
-            c1(j - L_C1)
-            outc(j - L_OUT, False)
-            store(j - L_OUT)
-            r_add(j + A_R)
-            v5(j + A_V5)
-            wt(j + A_V5)
-            r_rec(j + A_R)
-            q1(j - L_Q1)
-            mm2(j - L_Q1)
+            outc(j - 2, True)
+            c1(j)
+            r_add(j + 2)
+            r_rec(j + 2)
+            v5(j + 1, 0)
+            v5(j + 1, 1)
+            wt(j + 1)
+            outc(j - 2, False)
+            store(j - 2)
+            q1(j)
+            mm2(j)

@@ -38,7 +38,7 @@ def x_on_scalar(g, h):
 
 
 def v5_on_gpsimd(j):
-    return True
+    return False
 
 
 def out_on_scalar(t):
@@ -174,14 +174,14 @@ def tile_multiscalegeometricattention_t_kernel(tc, x, positions, values, tempera
                 )
 
         def clamp_v(g, q):
-            if g < NG and not (q == 3 and g < NG - 1):
+            if g < NG :
                 nc.vector.tensor_scalar(
                     out=zz[:, g % NZ, q, :], in0=zz[:, g % NZ, q, :], scalar1=-TINY, scalar2=t_b[:, q : q + 1],
                     op0=ALU.min, op1=ALU.mult,
                 )
 
         def clamp_g(g, q):
-            if g < NG and not (q == 3 and g == NG - 1):
+            if g < NG and False:
                 nc.gpsimd.tensor_scalar(
                     out=zz[:, g % NZ, q, :], in0=zz[:, g % NZ, q, :], scalar1=-TINY, scalar2=-BIG,
                     op0=ALU.min, op1=ALU.max,
@@ -348,6 +348,7 @@ def tile_multiscalegeometricattention_t_kernel(tc, x, positions, values, tempera
             sq(g - 1, 3)
             bc(g + 2)
             qx(g + 1)
+            clamp_v(g, 2)
             clamp_v(g, 3)
             clamp_v(g, 0)
             xcopy(g + 2, 1, False)

@@ -21,7 +21,7 @@ NP = NT // 2
 NG = NT // 4
 FLOPS = 2 * 2 * ROWS * D * N
 
-NX = 7
+NX = 6
 LN = 3
 NZ = 2
 NW = 3
@@ -33,8 +33,12 @@ TINY = 1.0e-30
 BIG = 3.0e38
 
 
+def gp(q):
+    return False
+
+
 def x_on_scalar(g, h):
-    return h == 1 and g % 2 == 1
+    return h == 1 and g != 0 and g != 2
 
 
 def v5_on_gpsimd(j):
@@ -57,9 +61,9 @@ def tile_multiscalegeometricattention_t_kernel(tc, x, positions, values, tempera
         x_sb = sb.tile([P, NX, 4, D], BF16, name="x_sb")
         v = sb.tile([P, NT, N], F32, name="v")
         xg = sb.tile([P, 2, 4 * D], BF16, name="xg", align_bytes=64)
-        xc = sb.tile([P, 2, D], U32, name="xc", align_bytes=64)
-        xs = sb.tile([P, 2, D], U8, name="xs", align_bytes=64)
-        xb = sb.tile([P, 2, D], F32, name="xb")
+        xc = sb.tile([P, 3, D], U32, name="xc", align_bytes=64)
+        xs = sb.tile([P, 3, D], U8, name="xs", align_bytes=64)
+        xb = sb.tile([P, 3, D], F32, name="xb")
         zz = sb.tile([P, NZ, 4, D], F32, name="zz")
         posc = sb.tile([P, N], U32, name="posc", align_bytes=64)
         poss = sb.tile([P, N], U8, name="poss", align_bytes=64)
@@ -81,8 +85,6 @@ def tile_multiscalegeometricattention_t_kernel(tc, x, positions, values, tempera
         t_a = sb.tile([P, 4], F32, name="t_a")
         t_b = sb.tile([P, 4], F32, name="t_b")
         idf = sb.tile([P, P], F32, name="idf")
-        junk = sb.tile([P, D], BF16, name="junk")
-        junk_v = sb.tile([P, D], BF16, name="junk_v")
         p2h_v = sb.tile([P, 2], F32, name="p2h_v")
         one = sb.tile([P, 1], F32, name="one")
         one2 = sb.tile([P, 1], F32, name="one2")
@@ -95,6 +97,8 @@ def tile_multiscalegeometricattention_t_kernel(tc, x, positions, values, tempera
         wb32 = wb[:].bitcast(F32)
         wg32 = wg[:].bitcast(F32)
         half = math.sqrt(0.5)
+        junk = wb[:, 0, 0, :]
+        junk_v = wb[:, 0, 1, :]
 
         def load_x(g):
             if g < NG:
@@ -102,9 +106,8 @@ def tile_multiscalegeometricattention_t_kernel(tc, x, positions, values, tempera
 
         def sq_norm(g, i):
             if g < NG:
-                t = 4 * g + i
                 nc.scalar.activation(
-                    out=junk[:], in_=x_sb[:, g % NX, i, :], func=ACT.Square, scale=half, accum_out=x2h[:, t : t + 1]
+                    out=junk, in_=x_sb[:, g % NX, i, :], func=ACT.Square, scale=half, accum_out=x2h[:, 4 * g + i : 4 * g + i + 1]
                 )
 
         def word_transposes(bank, src32):
@@ -125,7 +128,7 @@ def tile_multiscalegeometricattention_t_kernel(tc, x, positions, values, tempera
             return banks[(3 * g + k) % 2]
 
         def xbank(g, h):
-            return banks[2 + h] if g == 1 else tbank(g - 1, 1 + h)
+            return banks[(2 * g if g < 2 else 6) + h] if g < 3 else tbank(g - 3, 2 * h)
 
         def xt(g, h):
             if g < NG:
@@ -139,29 +142,32 @@ def tile_multiscalegeometricattention_t_kernel(tc, x, positions, values, tempera
 
         def qx(g):
             if g < NG:
-                nc.vector.quantize_mx(out=xc[:, g % 2, :].bitcast(FP8X4), scales=xs[:, g % 2, :], in_=xg[:, g % 2, :])
+                nc.vector.quantize_mx(out=xc[:, g % 3, :].bitcast(FP8X4), scales=xs[:, g % 3, :], in_=xg[:, g % 2, :])
+
+        def bbank(g):
+            return banks[g % 2] if g < 2 else tbank(g - 2, 1)
 
         def bc(g):
             if g < NG:
                 for i in range(4):
                     t = 4 * g + i
                     nc.tensor.transpose(
-                        tbank(g, 0)[:, i * P : (i + 1) * P], x2h[:, t : t + 1].to_broadcast([P, P]), idf[:]
+                        bbank(g)[:, i * P : (i + 1) * P], x2h[:, t : t + 1].to_broadcast([P, P]), idf[:]
                     )
 
         def bcopy(g):
             if g < NG:
-                nc.vector.tensor_copy(out=xb[:, g % 2, :], in_=tbank(g, 0)[:])
+                nc.vector.tensor_copy(out=xb[:, g % 3, :], in_=bbank(g)[:])
 
-        def mm1(g):
+        def mm1(g, qs):
             if g < NG:
-                for q in (2, 3, 0, 1):
+                for q in qs:
                     nc.tensor.matmul_mx(
                         out=banks[2 + q][:],
                         lhsT=posc[:, q * P : (q + 1) * P].bitcast(FP8X4),
                         lhsT_scale=poss[:, q * P : (q + 1) * P],
-                        rhs=xc[:, g % 2, :].bitcast(FP8X4),
-                        rhs_scale=xs[:, g % 2, :],
+                        rhs=xc[:, g % 3, :].bitcast(FP8X4),
+                        rhs_scale=xs[:, g % 3, :],
                         start=True,
                         stop=True,
                     )
@@ -169,19 +175,19 @@ def tile_multiscalegeometricattention_t_kernel(tc, x, positions, values, tempera
         def dist(g, q):
             if g < NG:
                 nc.vector.scalar_tensor_tensor(
-                    out=zz[:, g % NZ, q, :], in0=banks[2 + q][:], scalar=(p2h[:, q : q + 1] if q < 2 else p2h_v[:, q - 2 : q - 1]), in1=xb[:, g % 2, :],
+                    out=zz[:, g % NZ, q, :], in0=banks[2 + q][:], scalar=(p2h[:, q : q + 1] if q < 2 else p2h_v[:, q - 2 : q - 1]), in1=xb[:, g % 3, :],
                     op0=ALU.subtract, op1=ALU.subtract,
                 )
 
         def clamp_v(g, q):
-            if g < NG :
+            if g < NG and not gp(q):
                 nc.vector.tensor_scalar(
                     out=zz[:, g % NZ, q, :], in0=zz[:, g % NZ, q, :], scalar1=-TINY, scalar2=t_b[:, q : q + 1],
                     op0=ALU.min, op1=ALU.mult,
                 )
 
         def clamp_g(g, q):
-            if g < NG and False:
+            if g < NG and gp(q):
                 nc.gpsimd.tensor_scalar(
                     out=zz[:, g % NZ, q, :], in0=zz[:, g % NZ, q, :], scalar1=-TINY, scalar2=-BIG,
                     op0=ALU.min, op1=ALU.max,
@@ -292,7 +298,7 @@ def tile_multiscalegeometricattention_t_kernel(tc, x, positions, values, tempera
         xt(0, 0)
         xt(0, 1)
         for c in range(2):
-            nc.scalar.activation(out=junk[:], in_=pos_sb[:, c, :], func=ACT.Square, scale=half, accum_out=p2h[:, c : c + 1])
+            nc.scalar.activation(out=junk, in_=pos_sb[:, c, :], func=ACT.Square, scale=half, accum_out=p2h[:, c : c + 1])
         for i in range(4):
             sq_norm(0, i)
         for h in range(2):
@@ -304,7 +310,7 @@ def tile_multiscalegeometricattention_t_kernel(tc, x, positions, values, tempera
         qx(0)
         for c in range(2, 4):
             nc.vector.scalar_tensor_tensor(
-                out=junk_v[:], in0=pos_sb[:, c, :], scalar=0.5, in1=pos_sb[:, c, :], op0=ALU.mult, op1=ALU.mult,
+                out=junk_v, in0=pos_sb[:, c, :], scalar=0.5, in1=pos_sb[:, c, :], op0=ALU.mult, op1=ALU.mult,
                 accum_out=p2h_v[:, c - 2 : c - 1],
             )
         xt(1, 0)
@@ -315,46 +321,52 @@ def tile_multiscalegeometricattention_t_kernel(tc, x, positions, values, tempera
                 sq_norm(g, i)
             if g == 1:
                 xcopy(1, 1, True)
-        xcopy(1, 0, False)
-        xcopy(1, 1, False)
+        xcopy(1, 0)
         bc(1)
+        xt(2, 0)
+        xt(2, 1)
 
         for g in range(NG + 1):
             if g >= 1:
                 load_x(g - 1 + NX)
             if g == 2:
                 nc.sync.dma_start(out=pos_sb[:], in_=values.rearrange("(p c) d -> p c d", c=4))
-            mm1(g)
+            if g == 0:
+                mm1(0, (2, 3, 0, 1))
+                bcopy(1)
+                xt(3, 0)
             zt(g - 1, 0)
             zt(g - 1, 1)
-            xt(g + 2, 0)
+            bc(g + 2)
             sq_norm(g + LN, 0)
-            sq(g - 1, 0)
             sq_norm(g + LN, 1)
+            sq(g - 1, 0)
+            sq_norm(g + LN, 2)
             sq(g - 1, 1)
             for q in (2, 3):
                 dist(g, q)
                 clamp_g(g, q)
-            bcopy(g + 1)
-            xcopy(g + 2, 0, False)
-            xt(g + 2, 1)
+            if g == 0:
+                xcopy(2, 0)
+                xcopy(2, 1)
+                qx(1)
+            xcopy(g + 3, 0)
+            xt(g + 3, 1)
             zt(g - 1, 2)
-            sq_norm(g + LN, 2)
+            sq_norm(g + LN, 3)
             sq(g - 1, 2)
             dist(g, 0)
             dist(g, 1)
+            mm1(g + 1, (2, 3))
             zt(g - 1, 3)
-            sq_norm(g + LN, 3)
+            bcopy(g + 2)
+            xcopy(g + 3, 1)
             sq(g - 1, 3)
-            bc(g + 2)
-            qx(g + 1)
-            clamp_v(g, 2)
-            clamp_v(g, 3)
-            clamp_v(g, 0)
-            xcopy(g + 2, 1, False)
-            clamp_v(g, 1)
-            xcopy(g + 2, 0, True)
-            xcopy(g + 2, 1, True)
+            qx(g + 2)
+            for q in range(4):
+                clamp_v(g, q)
+            mm1(g + 1, (0, 1))
+            xt(g + 4, 0)
             if g == NG - 1:
                 nc.vector.tensor_copy(
                     out=pg[:].rearrange("p (d c) -> p d c", c=4), in_=pos_sb[:].rearrange("p c d -> p d c")

@@ -28,7 +28,7 @@ NW = 3
 NO = 4
 WT = 3
 SB = 8 - WT
-A_EX = 3
+A_EX = 5
 TINY = 1.0e-30
 BIG = 3.0e38
 
@@ -216,15 +216,12 @@ def tile_multiscalegeometricattention_t_kernel(tc, x, positions, values, tempera
                     )
 
         def r_add(j):
-            if 0 <= j < NP:
-                nc.gpsimd.tensor_scalar(
-                    out=ra[:, 2 * j : 2 * j + 2], in0=sums[:, 2 * j : 2 * j + 2], scalar1=1.0e-8, scalar2=1.0,
-                    op0=ALU.add, op1=ALU.mult,
-                )
+            if 0 <= j < NP and j % 2 == 0:
+                nc.vector.tensor_scalar_add(out=ra[:, 2 * j : 2 * j + 4], in0=sums[:, 2 * j : 2 * j + 4], scalar1=1.0e-8)
 
         def r_rec(j):
-            if 0 <= j < NP:
-                nc.vector.reciprocal(out=rr[:, 2 * j : 2 * j + 2], in_=ra[:, 2 * j : 2 * j + 2])
+            if 0 <= j < NP and j % 2 == 0:
+                nc.vector.reciprocal(out=rr[:, 2 * j : 2 * j + 4], in_=ra[:, 2 * j : 2 * j + 4])
 
         def v5(j, i):
             if 0 <= j < NP:
@@ -242,7 +239,7 @@ def tile_multiscalegeometricattention_t_kernel(tc, x, positions, values, tempera
 
         def c1(j):
             if 0 <= j < NP:
-                word_copy(wg32[:, j % NW, :], banks[j % WT], j >= NP - 2)
+                word_copy(wg32[:, j % NW, :], banks[j % WT], j >= NP - 5)
 
         def q1(j):
             if 0 <= j < NP:
@@ -285,14 +282,6 @@ def tile_multiscalegeometricattention_t_kernel(tc, x, positions, values, tempera
         for g in range(NX):
             load_x(g)
 
-        nc.vector.tensor_copy(out=t_a[:], in_=t_bf[:])
-        nc.vector.tensor_scalar_mul(out=t_b[:], in0=t_a[:], scalar1=-1.0)
-        nc.vector.tensor_tensor(out=t_a[:], in0=t_a[:], in1=t_b[:], op=ALU.max)
-        nc.vector.tensor_scalar(out=t_a[:], in0=t_a[:], scalar1=0.1, scalar2=0.05, op0=ALU.add, op1=ALU.mult)
-        nc.vector.tensor_tensor(out=t_a[:], in0=t_a[:], in1=t_a[:], op=ALU.mult)
-        nc.vector.reciprocal(out=t_b[:], in_=t_a[:])
-        nc.vector.tensor_scalar_mul(out=t_b[:], in0=t_b[:], scalar1=-2.0)
-
         for h in range(2):
             word_transposes(banks[2 + h], lambda i: pos32[:, 2 * h + i, :])
         xt(0, 0)
@@ -301,18 +290,25 @@ def tile_multiscalegeometricattention_t_kernel(tc, x, positions, values, tempera
             nc.scalar.activation(out=junk, in_=pos_sb[:, c, :], func=ACT.Square, scale=half, accum_out=p2h[:, c : c + 1])
         for i in range(4):
             sq_norm(0, i)
-        for h in range(2):
-            word_copy(pg32[:, h * 512 : (h + 1) * 512], banks[2 + h])
+        word_copy(pg32[:, :512], banks[2])
+        nc.vector.tensor_copy(out=t_a[:], in_=t_bf[:])
+        word_copy(pg32[:, 512:], banks[3])
+        nc.vector.tensor_scalar_mul(out=t_b[:], in0=t_a[:], scalar1=-1.0)
         xcopy(0, 0)
+        nc.vector.tensor_tensor(out=t_a[:], in0=t_a[:], in1=t_b[:], op=ALU.max)
         xcopy(0, 1)
+        nc.vector.tensor_scalar(out=t_a[:], in0=t_a[:], scalar1=0.1, scalar2=0.05, op0=ALU.add, op1=ALU.mult)
         nc.vector.quantize_mx(out=posc[:].bitcast(FP8X4), scales=poss[:], in_=pg[:])
+        nc.vector.tensor_tensor(out=t_a[:], in0=t_a[:], in1=t_a[:], op=ALU.mult)
         bc(0)
         qx(0)
+        nc.vector.reciprocal(out=t_b[:], in_=t_a[:])
         for c in range(2, 4):
             nc.vector.scalar_tensor_tensor(
                 out=junk_v, in0=pos_sb[:, c, :], scalar=0.5, in1=pos_sb[:, c, :], op0=ALU.mult, op1=ALU.mult,
                 accum_out=p2h_v[:, c - 2 : c - 1],
             )
+        nc.vector.tensor_scalar_mul(out=t_b[:], in0=t_b[:], scalar1=-2.0)
         xt(1, 0)
         xt(1, 1)
         bcopy(0)
@@ -377,13 +373,13 @@ def tile_multiscalegeometricattention_t_kernel(tc, x, positions, values, tempera
         for j in range(-A_EX, NP + 3):
             ex(j + A_EX)
             outc(j - 2, True)
-            c1(j)
             r_add(j + 2)
+            c1(j)
             r_rec(j + 2)
-            v5(j + 1, 0)
-            v5(j + 1, 1)
-            wt(j + 1)
             outc(j - 2, False)
+            v5(j + 2, 0)
+            v5(j + 2, 1)
+            wt(j + 2)
             store(j - 2)
             q1(j)
             mm2(j)

@@ -29,12 +29,8 @@ NO = 4
 WT = 3
 SB = 8 - WT
 A_EX = 5
+TC = 6
 TINY = 1.0e-30
-BIG = 3.0e38
-
-
-def gp(q):
-    return False
 
 
 def x_on_scalar(g, h):
@@ -46,7 +42,7 @@ def v5_on_gpsimd(j):
 
 
 def out_on_scalar(t):
-    return t % 2 == 0 or t % 8 == 7
+    return t % 2 == 0 or (t % 8 == 3 and t < NT - 8)
 
 
 def tile_multiscalegeometricattention_t_kernel(tc, x, positions, values, temperature, out):
@@ -180,21 +176,10 @@ def tile_multiscalegeometricattention_t_kernel(tc, x, positions, values, tempera
                 )
 
         def clamp_v(g, q):
-            if g < NG and not gp(q):
+            if g < NG:
                 nc.vector.tensor_scalar(
                     out=zz[:, g % NZ, q, :], in0=zz[:, g % NZ, q, :], scalar1=-TINY, scalar2=t_b[:, q : q + 1],
                     op0=ALU.min, op1=ALU.mult,
-                )
-
-        def clamp_g(g, q):
-            if g < NG and gp(q):
-                nc.gpsimd.tensor_scalar(
-                    out=zz[:, g % NZ, q, :], in0=zz[:, g % NZ, q, :], scalar1=-TINY, scalar2=-BIG,
-                    op0=ALU.min, op1=ALU.max,
-                )
-                nc.gpsimd.tensor_scalar(
-                    out=zz[:, g % NZ, q, :], in0=zz[:, g % NZ, q, :], scalar1=t_b[:, q : q + 1], scalar2=1.0,
-                    op0=ALU.mult, op1=ALU.mult,
                 )
 
         def zt(g, i):
@@ -215,13 +200,20 @@ def tile_multiscalegeometricattention_t_kernel(tc, x, positions, values, tempera
                         out=v[:, t, :], in_=v[:, t, :], func=ACT.Exp, scale=-1.0, accum_out=sums[:, t : t + 1]
                     )
 
+        def r_tiles(j):
+            if not 0 <= j < NP:
+                return 0
+            return 2 if j < 2 else 4 * (1 - j % 2)
+
         def r_add(j):
-            if 0 <= j < NP and j % 2 == 0:
-                nc.vector.tensor_scalar_add(out=ra[:, 2 * j : 2 * j + 4], in0=sums[:, 2 * j : 2 * j + 4], scalar1=1.0e-8)
+            n = r_tiles(j)
+            if n:
+                nc.vector.tensor_scalar_add(out=ra[:, 2 * j : 2 * j + n], in0=sums[:, 2 * j : 2 * j + n], scalar1=1.0e-8)
 
         def r_rec(j):
-            if 0 <= j < NP and j % 2 == 0:
-                nc.vector.reciprocal(out=rr[:, 2 * j : 2 * j + 4], in_=ra[:, 2 * j : 2 * j + 4])
+            n = r_tiles(j)
+            if n:
+                nc.vector.reciprocal(out=rr[:, 2 * j : 2 * j + n], in_=ra[:, 2 * j : 2 * j + n])
 
         def v5(j, i):
             if 0 <= j < NP:
@@ -237,9 +229,9 @@ def tile_multiscalegeometricattention_t_kernel(tc, x, positions, values, tempera
             if 0 <= j < NP:
                 word_transposes(banks[j % WT], lambda i: wb32[:, j % NW, i, :])
 
-        def c1(j):
-            if 0 <= j < NP:
-                word_copy(wg32[:, j % NW, :], banks[j % WT], j >= NP - 5)
+        def c1(j, on_scalar):
+            if 0 <= j < NP and on_scalar == (j >= NP - TC):
+                word_copy(wg32[:, j % NW, :], banks[j % WT], on_scalar)
 
         def q1(j):
             if 0 <= j < NP:
@@ -272,14 +264,22 @@ def tile_multiscalegeometricattention_t_kernel(tc, x, positions, values, tempera
 
         def store(j):
             if 0 <= j < NP:
-                nc.sync.dma_start(out=ov[:, 2 * j : 2 * j + 2, :], in_=ob[:, j % NO, :, :])
+                if j < NP - 1:
+                    nc.sync.dma_start(out=ov[:, 2 * j : 2 * j + 2, :], in_=ob[:, j % NO, :, :])
+                else:
+                    for i in range(2):
+                        nc.sync.dma_start(out=ov[:, 2 * j + i : 2 * j + i + 1, :], in_=ob[:, j % NO, i : i + 1, :])
 
         nc.vector.memset(one[:], 1.0)
         nc.scalar.dma_start(out=t_bf[:], in_=temperature.rearrange("(p c) -> p c", c=4))
         nc.scalar.activation(out=one2[:], in_=one[:], func=ACT.Sqrt)
-        nc.sync.dma_start(out=pos_sb[:], in_=positions.rearrange("(p c) d -> p c d", c=4))
+        pos_v = positions.rearrange("(p c) d -> p c d", c=4)
+        for h in range(2):
+            nc.sync.dma_start(out=pos_sb[:, 2 * h : 2 * h + 2, :], in_=pos_v[:, 2 * h : 2 * h + 2, :])
         make_identity(nc, idf[:])
-        for g in range(NX):
+        for h in range(2):
+            nc.sync.dma_start(out=x_sb[:, 0, 2 * h : 2 * h + 2, :], in_=xv[:, 2 * h : 2 * h + 2, :])
+        for g in range(1, NX):
             load_x(g)
 
         for h in range(2):
@@ -341,7 +341,6 @@ def tile_multiscalegeometricattention_t_kernel(tc, x, positions, values, tempera
             sq(g - 1, 1)
             for q in (2, 3):
                 dist(g, q)
-                clamp_g(g, q)
             if g == 0:
                 xcopy(2, 0)
                 xcopy(2, 1)
@@ -371,10 +370,11 @@ def tile_multiscalegeometricattention_t_kernel(tc, x, positions, values, tempera
                 nc.vector.quantize_mx(out=valc[:].bitcast(FP8X4), scales=vals[:], in_=pg[:])
 
         for j in range(-A_EX, NP + 3):
+            c1(j, True)
             ex(j + A_EX)
             outc(j - 2, True)
             r_add(j + 2)
-            c1(j)
+            c1(j, False)
             r_rec(j + 2)
             outc(j - 2, False)
             v5(j + 2, 0)

@@ -25,7 +25,6 @@ NX = 6
 LN = 3
 NZ = 2
 NW = 3
-NO = 4
 WT = 3
 SB = 8 - WT
 A_EX = 5
@@ -56,7 +55,7 @@ def tile_multiscalegeometricattention_t_kernel(tc, x, positions, values, tempera
 
         x_sb = sb.tile([P, NX, 4, D], BF16, name="x_sb")
         v = sb.tile([P, NT, N], F32, name="v")
-        xg = sb.tile([P, 2, 4 * D], BF16, name="xg", align_bytes=64)
+        xg = sb.tile([P, 3, 4 * D], BF16, name="xg", align_bytes=64)
         xc = sb.tile([P, 3, D], U32, name="xc", align_bytes=64)
         xs = sb.tile([P, 3, D], U8, name="xs", align_bytes=64)
         xb = sb.tile([P, 3, D], F32, name="xb")
@@ -71,7 +70,7 @@ def tile_multiscalegeometricattention_t_kernel(tc, x, positions, values, tempera
         wg = sb.tile([P, NW, 1024], BF16, name="wg", align_bytes=64)
         wc = sb.tile([P, NW, 256], U32, name="wc", align_bytes=64)
         ws = sb.tile([P, NW, 256], U8, name="ws", align_bytes=64)
-        ob = sb.tile([P, NO, 2, D], F32, name="ob")
+        junk = sb.tile([P, 12, D], BF16, name="junk")
         x2h = sb.tile([P, NT], F32, name="x2h")
         sums = sb.tile([P, NT], F32, name="sums")
         rr = sb.tile([P, NT], F32, name="rr")
@@ -93,7 +92,6 @@ def tile_multiscalegeometricattention_t_kernel(tc, x, positions, values, tempera
         wb32 = wb[:].bitcast(F32)
         wg32 = wg[:].bitcast(F32)
         half = math.sqrt(0.5)
-        junk = wb[:, 0, 0, :]
         junk_v = wb[:, 0, 1, :]
 
         def load_x(g):
@@ -103,7 +101,7 @@ def tile_multiscalegeometricattention_t_kernel(tc, x, positions, values, tempera
         def sq_norm(g, i):
             if g < NG:
                 nc.scalar.activation(
-                    out=junk, in_=x_sb[:, g % NX, i, :], func=ACT.Square, scale=half, accum_out=x2h[:, 4 * g + i : 4 * g + i + 1]
+                    out=junk[:, (4 * g + i) % 12, :], in_=x_sb[:, g % NX, i, :], func=ACT.Square, scale=half, accum_out=x2h[:, 4 * g + i : 4 * g + i + 1]
                 )
 
         def word_transposes(bank, src32):
@@ -134,11 +132,11 @@ def tile_multiscalegeometricattention_t_kernel(tc, x, positions, values, tempera
             if g < NG:
                 s = x_on_scalar(g, h)
                 if on_scalar is None or s == on_scalar:
-                    word_copy(xg32[:, g % 2, h * 512 : (h + 1) * 512], xbank(g, h), s)
+                    word_copy(xg32[:, g % 3, h * 512 : (h + 1) * 512], xbank(g, h), s)
 
         def qx(g):
             if g < NG:
-                nc.vector.quantize_mx(out=xc[:, g % 3, :].bitcast(FP8X4), scales=xs[:, g % 3, :], in_=xg[:, g % 2, :])
+                nc.vector.quantize_mx(out=xc[:, g % 3, :].bitcast(FP8X4), scales=xs[:, g % 3, :], in_=xg[:, g % 3, :])
 
         def bbank(g):
             return banks[g % 2] if g < 2 else tbank(g - 2, 1)
@@ -258,17 +256,17 @@ def tile_multiscalegeometricattention_t_kernel(tc, x, positions, values, tempera
                     if out_on_scalar(t) != on_scalar:
                         continue
                     if on_scalar:
-                        nc.scalar.copy(out=ob[:, j % NO, i, :], in_=banks[WT + t % SB][:])
+                        nc.scalar.copy(out=v[:, t, :], in_=banks[WT + t % SB][:])
                     else:
-                        nc.vector.tensor_copy(out=ob[:, j % NO, i, :], in_=banks[WT + t % SB][:])
+                        nc.vector.tensor_copy(out=v[:, t, :], in_=banks[WT + t % SB][:])
 
         def store(j):
             if 0 <= j < NP:
                 if j < NP - 1:
-                    nc.sync.dma_start(out=ov[:, 2 * j : 2 * j + 2, :], in_=ob[:, j % NO, :, :])
+                    nc.sync.dma_start(out=ov[:, 2 * j : 2 * j + 2, :], in_=v[:, 2 * j : 2 * j + 2, :])
                 else:
-                    for i in range(2):
-                        nc.sync.dma_start(out=ov[:, 2 * j + i : 2 * j + i + 1, :], in_=ob[:, j % NO, i : i + 1, :])
+                    for t in (2 * j, 2 * j + 1):
+                        nc.sync.dma_start(out=ov[:, t : t + 1, :], in_=v[:, t : t + 1, :])
 
         nc.vector.memset(one[:], 1.0)
         nc.scalar.dma_start(out=t_bf[:], in_=temperature.rearrange("(p c) -> p c", c=4))
@@ -287,7 +285,7 @@ def tile_multiscalegeometricattention_t_kernel(tc, x, positions, values, tempera
         xt(0, 0)
         xt(0, 1)
         for c in range(2):
-            nc.scalar.activation(out=junk, in_=pos_sb[:, c, :], func=ACT.Square, scale=half, accum_out=p2h[:, c : c + 1])
+            nc.scalar.activation(out=junk[:, 8 + c, :], in_=pos_sb[:, c, :], func=ACT.Square, scale=half, accum_out=p2h[:, c : c + 1])
         for i in range(4):
             sq_norm(0, i)
         word_copy(pg32[:, :512], banks[2])

import math
from contextlib import ExitStack

import concourse.mybir as mybir
from concourse.masks import make_identity

F32 = mybir.dt.float32
BF16 = mybir.dt.bfloat16
U32 = mybir.dt.uint32
U8 = mybir.dt.uint8
FP8X4 = mybir.dt.float8_e4m3fn_x4
ALU = mybir.AluOpType
ACT = mybir.ActivationFunctionType

P = 128
D = 512
N = 512
ROWS = 8192
NT = ROWS // P
NP = NT // 2
NG = NT // 4
FLOPS = 2 * 2 * ROWS * D * N

NX = 6
LN = 3
NZ = 2
NW = 3
WT = 3
SB = 8 - WT
A_EX = 5
TC = 6
TINY = 1.0e-30


def x_on_scalar(g, h):
    return h == 1 and g != 0 and g != 2


def v5_on_gpsimd(j):
    return False


def out_on_scalar(t):
    return t % 2 == 0 or (t % 8 == 3 and t < NT - 8)


def tile_multiscalegeometricattention_t_kernel(tc, x, positions, values, temperature, out):
    nc = tc.nc
    xv = x.flatten_outer_dims().rearrange("(p t) d -> p t d", t=NT)
    ov = out.flatten_outer_dims().rearrange("(p t) d -> p t d", t=NT)
    with ExitStack() as ctx:
        sb = ctx.enter_context(tc.tile_pool(name="sb", bufs=1))
        ps = ctx.enter_context(tc.psum_pool(name="ps", bufs=1))
        ctx.enter_context(tc.manual_schedule())

        x_sb = sb.tile([P, NX, 4, D], BF16, name="x_sb")
        v = sb.tile([P, NT, N], F32, name="v")
        xg = sb.tile([P, 3, 4 * D], BF16, name="xg", align_bytes=64)
        xc = sb.tile([P, 3, D], U32, name="xc", align_bytes=64)
        xs = sb.tile([P, 3, D], U8, name="xs", align_bytes=64)
        xb = sb.tile([P, 3, D], F32, name="xb")
        zz = sb.tile([P, NZ, 4, D], F32, name="zz")
        posc = sb.tile([P, N], U32, name="posc", align_bytes=64)
        poss = sb.tile([P, N], U8, name="poss", align_bytes=64)
        valc = sb.tile([P, D], U32, name="valc", align_bytes=64)
        vals = sb.tile([P, D], U8, name="vals", align_bytes=64)
        pos_sb = sb.tile([P, 4, D], BF16, name="pos_sb")
        pg = sb.tile([P, 4 * D], BF16, name="pg", align_bytes=64)
        wb = sb.tile([P, NW, 2, N], BF16, name="wb")
        wg = sb.tile([P, NW, 1024], BF16, name="wg", align_bytes=64)
        wc = sb.tile([P, NW, 256], U32, name="wc", align_bytes=64)
        ws = sb.tile([P, NW, 256], U8, name="ws", align_bytes=64)
        junk = sb.tile([P, 12, D], BF16, name="junk")
        x2h = sb.tile([P, NT], F32, name="x2h")
        sums = sb.tile([P, NT], F32, name="sums")
        rr = sb.tile([P, NT], F32, name="rr")
        ra = sb.tile([P, NT], F32, name="ra")
        p2h = sb.tile([P, 4], F32, name="p2h")
        t_bf = sb.tile([P, 4], BF16, name="t_bf")
        t_a = sb.tile([P, 4], F32, name="t_a")
        t_b = sb.tile([P, 4], F32, name="t_b")
        idf = sb.tile([P, P], F32, name="idf")
        p2h_v = sb.tile([P, 2], F32, name="p2h_v")
        one = sb.tile([P, 1], F32, name="one")
        one2 = sb.tile([P, 1], F32, name="one2")
        banks = [ps.tile([P, 512], F32, name="bank%d" % b) for b in range(8)]

        x32 = x_sb[:].bitcast(F32)
        xg32 = xg[:].bitcast(F32)
        pos32 = pos_sb[:].bitcast(F32)
        pg32 = pg[:].bitcast(F32)
        wb32 = wb[:].bitcast(F32)
        wg32 = wg[:].bitcast(F32)
        half = math.sqrt(0.5)
        junk_v = wb[:, 0, 1, :]

        def load_x(g):
            if g < NG:
                nc.sync.dma_start(out=x_sb[:, g % NX, :, :], in_=xv[:, 4 * g : 4 * g + 4, :])

        def sq_norm(g, i):
            if g < NG:
                nc.scalar.activation(
                    out=junk[:, (4 * g + i) % 12, :], in_=x_sb[:, g % NX, i, :], func=ACT.Square, scale=half, accum_out=x2h[:, 4 * g + i : 4 * g + i + 1]
                )

        def word_transposes(bank, src32):
            for i in range(2):
                for u in range(2):
                    q = 2 * i + u
                    nc.tensor.transpose(bank[:, q * P : (q + 1) * P], src32(i)[:, u * P : (u + 1) * P], idf[:])

        def word_copy(dst32, bank, on_scalar=False):
            src = bank[:].rearrange("p (i u r) -> p i r u", i=2, u=2)
            dst = dst32.rearrange("p (i r u) -> p i r u", i=2, u=2)
            if on_scalar:
                nc.scalar.copy(out=dst, in_=src)
            else:
                nc.vector.tensor_copy(out=dst, in_=src)

        def tbank(g, k):
            return banks[(3 * g + k) % 2]

        def xbank(g, h):
            return banks[(2 * g if g < 2 else 6) + h] if g < 3 else tbank(g - 3, 2 * h)

        def xt(g, h):
            if g < NG:
                word_transposes(xbank(g, h), lambda i: x32[:, g % NX, 2 * h + i, :])

        def xcopy(g, h, on_scalar=None):
            if g < NG:
                s = x_on_scalar(g, h)
                if on_scalar is None or s == on_scalar:
                    word_copy(xg32[:, g % 3, h * 512 : (h + 1) * 512], xbank(g, h), s)

        def qx(g):
            if g < NG:
                nc.vector.quantize_mx(out=xc[:, g % 3, :].bitcast(FP8X4), scales=xs[:, g % 3, :], in_=xg[:, g % 3, :])

        def bbank(g):
            return banks[g % 2] if g < 2 else tbank(g - 2, 1)

        def bc(g):
            if g < NG:
                for i in range(4):
                    t = 4 * g + i
                    nc.tensor.transpose(
                        bbank(g)[:, i * P : (i + 1) * P], x2h[:, t : t + 1].to_broadcast([P, P]), idf[:]
                    )

        def bcopy(g):
            if g < NG:
                nc.vector.tensor_copy(out=xb[:, g % 3, :], in_=bbank(g)[:])

        def mm1(g, qs):
            if g < NG:
                for q in qs:
                    nc.tensor.matmul_mx(
                        out=banks[2 + q][:],
                        lhsT=posc[:, q * P : (q + 1) * P].bitcast(FP8X4),
                        lhsT_scale=poss[:, q * P : (q + 1) * P],
                        rhs=xc[:, g % 3, :].bitcast(FP8X4),
                        rhs_scale=xs[:, g % 3, :],
                        start=True,
                        stop=True,
                    )

        def dist(g, q):
            if g < NG:
                nc.vector.scalar_tensor_tensor(
                    out=zz[:, g % NZ, q, :], in0=banks[2 + q][:], scalar=(p2h[:, q : q + 1] if q < 2 else p2h_v[:, q - 2 : q - 1]), in1=xb[:, g % 3, :],
                    op0=ALU.subtract, op1=ALU.subtract,
                )

        def clamp_v(g, q):
            if g < NG:
                nc.vector.tensor_scalar(
                    out=zz[:, g % NZ, q, :], in0=zz[:, g % NZ, q, :], scalar1=-TINY, scalar2=t_b[:, q : q + 1],
                    op0=ALU.min, op1=ALU.mult,
                )

        def zt(g, i):
            if 0 <= g < NG:
                for q in range(4):
                    nc.tensor.transpose(
                        banks[6 + i % 2][:, q * P : (q + 1) * P], zz[:, g % NZ, q, i * P : (i + 1) * P], idf[:]
                    )

        def sq(g, i):
            if 0 <= g < NG:
                nc.scalar.activation(out=v[:, 4 * g + i, :], in_=banks[6 + i % 2][:], func=ACT.Sqrt)

        def ex(j):
            if 0 <= j < NP:
                for t in (2 * j, 2 * j + 1):
                    nc.scalar.activation(
                        out=v[:, t, :], in_=v[:, t, :], func=ACT.Exp, scale=-1.0, accum_out=sums[:, t : t + 1]
                    )

        def r_tiles(j):
            if not 0 <= j < NP:
                return 0
            return 2 if j < 2 else 4 * (1 - j % 2)

        def r_add(j):
            n = r_tiles(j)
            if n:
                nc.vector.tensor_scalar_add(out=ra[:, 2 * j : 2 * j + n], in0=sums[:, 2 * j : 2 * j + n], scalar1=1.0e-8)

        def r_rec(j):
            n = r_tiles(j)
            if n:
                nc.vector.reciprocal(out=rr[:, 2 * j : 2 * j + n], in_=ra[:, 2 * j : 2 * j + n])

        def v5(j, i):
            if 0 <= j < NP:
                t = 2 * j + i
                o = wb[:, j % NW, i, :].rearrange("p (u m e) -> p u m e", u=2, e=2)
                a = v[:, t, :].rearrange("p (u e m) -> p u m e", u=2, e=2)
                if i == 0 and v5_on_gpsimd(j):
                    nc.gpsimd.tensor_scalar(out=o, in0=a, scalar1=rr[:, t : t + 1], scalar2=1.0, op0=ALU.mult, op1=ALU.mult)
                else:
                    nc.vector.tensor_scalar_mul(out=o, in0=a, scalar1=rr[:, t : t + 1])

        def wt(j):
            if 0 <= j < NP:
                word_transposes(banks[j % WT], lambda i: wb32[:, j % NW, i, :])

        def c1(j, on_scalar):
            if 0 <= j < NP and on_scalar == (j >= NP - TC):
                word_copy(wg32[:, j % NW, :], banks[j % WT], on_scalar)

        def q1(j):
            if 0 <= j < NP:
                nc.vector.quantize_mx(out=wc[:, j % NW, :].bitcast(FP8X4), scales=ws[:, j % NW, :], in_=wg[:, j % NW, :])

        def mm2(j):
            if 0 <= j < NP:
                for i in range(2):
                    t = 2 * j + i
                    nc.tensor.matmul_mx(
                        out=banks[WT + t % SB][:],
                        lhsT=wc[:, j % NW, i * P : (i + 1) * P].bitcast(FP8X4),
                        lhsT_scale=ws[:, j % NW, i * P : (i + 1) * P],
                        rhs=valc[:].bitcast(FP8X4),
                        rhs_scale=vals[:],
                        start=True,
                        stop=True,
                    )

        def outc(j, on_scalar):
            if 0 <= j < NP:
                for i in range(2):
                    t = 2 * j + i
                    if out_on_scalar(t) != on_scalar:
                        continue
                    if on_scalar:
                        nc.scalar.copy(out=v[:, t, :], in_=banks[WT + t % SB][:])
                    else:
                        nc.vector.tensor_copy(out=v[:, t, :], in_=banks[WT + t % SB][:])

        def store(j):
            if 0 <= j < NP:
                if j < NP - 1:
                    nc.sync.dma_start(out=ov[:, 2 * j : 2 * j + 2, :], in_=v[:, 2 * j : 2 * j + 2, :])
                else:
                    for t in (2 * j, 2 * j + 1):
                        nc.sync.dma_start(out=ov[:, t : t + 1, :], in_=v[:, t : t + 1, :])

        nc.vector.memset(one[:], 1.0)
        nc.scalar.dma_start(out=t_bf[:], in_=temperature.rearrange("(p c) -> p c", c=4))
        nc.scalar.activation(out=one2[:], in_=one[:], func=ACT.Sqrt)
        pos_v = positions.rearrange("(p c) d -> p c d", c=4)
        for h in range(2):
            nc.sync.dma_start(out=pos_sb[:, 2 * h : 2 * h + 2, :], in_=pos_v[:, 2 * h : 2 * h + 2, :])
        make_identity(nc, idf[:])
        for h in range(2):
            nc.sync.dma_start(out=x_sb[:, 0, 2 * h : 2 * h + 2, :], in_=xv[:, 2 * h : 2 * h + 2, :])
        for g in range(1, NX):
            load_x(g)

        for h in range(2):
            word_transposes(banks[2 + h], lambda i: pos32[:, 2 * h + i, :])
        xt(0, 0)
        xt(0, 1)
        for c in range(2):
            nc.scalar.activation(out=junk[:, 8 + c, :], in_=pos_sb[:, c, :], func=ACT.Square, scale=half, accum_out=p2h[:, c : c + 1])
        for i in range(4):
            sq_norm(0, i)
        word_copy(pg32[:, :512], banks[2])
        nc.vector.tensor_copy(out=t_a[:], in_=t_bf[:])
        word_copy(pg32[:, 512:], banks[3])
        nc.vector.tensor_scalar_mul(out=t_b[:], in0=t_a[:], scalar1=-1.0)
        xcopy(0, 0)
        nc.vector.tensor_tensor(out=t_a[:], in0=t_a[:], in1=t_b[:], op=ALU.max)
        xcopy(0, 1)
        nc.vector.tensor_scalar(out=t_a[:], in0=t_a[:], scalar1=0.1, scalar2=0.05, op0=ALU.add, op1=ALU.mult)
        nc.vector.quantize_mx(out=posc[:].bitcast(FP8X4), scales=poss[:], in_=pg[:])
        nc.vector.tensor_tensor(out=t_a[:], in0=t_a[:], in1=t_a[:], op=ALU.mult)
        bc(0)
        qx(0)
        nc.vector.reciprocal(out=t_b[:], in_=t_a[:])
        for c in range(2, 4):
            nc.vector.scalar_tensor_tensor(
                out=junk_v, in0=pos_sb[:, c, :], scalar=0.5, in1=pos_sb[:, c, :], op0=ALU.mult, op1=ALU.mult,
                accum_out=p2h_v[:, c - 2 : c - 1],
            )
        nc.vector.tensor_scalar_mul(out=t_b[:], in0=t_b[:], scalar1=-2.0)
        xt(1, 0)
        xt(1, 1)
        bcopy(0)
        for g in range(1, LN):
            for i in range(4):
                sq_norm(g, i)
            if g == 1:
                xcopy(1, 1, True)
        xcopy(1, 0)
        bc(1)
        xt(2, 0)
        xt(2, 1)

        for g in range(NG + 1):
            if g >= 1:
                load_x(g - 1 + NX)
            if g == 2:
                nc.sync.dma_start(out=pos_sb[:], in_=values.rearrange("(p c) d -> p c d", c=4))
            if g == 0:
                mm1(0, (2, 3, 0, 1))
                bcopy(1)
                xt(3, 0)
            zt(g - 1, 0)
            zt(g - 1, 1)
            bc(g + 2)
            sq_norm(g + LN, 0)
            sq_norm(g + LN, 1)
            sq(g - 1, 0)
            sq_norm(g + LN, 2)
            sq(g - 1, 1)
            for q in (2, 3):
                dist(g, q)
            if g == 0:
                xcopy(2, 0)
                xcopy(2, 1)
                qx(1)
            xcopy(g + 3, 0)
            xt(g + 3, 1)
            zt(g - 1, 2)
            sq_norm(g + LN, 3)
            sq(g - 1, 2)
            dist(g, 0)
            dist(g, 1)
            mm1(g + 1, (2, 3))
            zt(g - 1, 3)
            bcopy(g + 2)
            xcopy(g + 3, 1)
            sq(g - 1, 3)
            qx(g + 2)
            for q in range(4):
                clamp_v(g, q)
            mm1(g + 1, (0, 1))
            xt(g + 4, 0)
            if g == NG - 1:
                nc.vector.tensor_copy(
                    out=pg[:].rearrange("p (d c) -> p d c", c=4), in_=pos_sb[:].rearrange("p c d -> p d c")
                )
            if g == NG:
                nc.vector.quantize_mx(out=valc[:].bitcast(FP8X4), scales=vals[:], in_=pg[:])

        for j in range(-A_EX, NP + 3):
            c1(j, True)
            ex(j + A_EX)
            outc(j - 2, True)
            r_add(j + 2)
            c1(j, False)
            r_rec(j + 2)
            outc(j - 2, False)
            v5(j + 2, 0)
            v5(j + 2, 1)
            wt(j + 2)
            store(j - 2)
            q1(j)
            mm2(j)
